import numpy as np
import ml_dtypes


def mxq(x, axis, fmt="e4m3"):
    dtype, down = {"e4m3": (ml_dtypes.float8_e4m3fn, 7), "e5m2": (ml_dtypes.float8_e5m2, 14)}[fmt]
    v = np.moveaxis(np.asarray(x, np.float32).astype(ml_dtypes.bfloat16).astype(np.float64), axis, -1)
    blocks = v.reshape(v.shape[:-1] + (-1, 32))
    amax = np.abs(blocks).max(-1, keepdims=True)
    byte = np.maximum(np.where(amax > 0, np.frexp(amax)[1] - 1 + 127, 0) - down, 1)
    scale = np.exp2(byte - 127.0)
    codes = (blocks / scale).astype(np.float32).astype(dtype).astype(np.float64)
    return np.moveaxis((codes * scale).reshape(v.shape), -1, axis)


WIDE = False


def mx_kscale(k):
    if not WIDE:
        return np.ones(k)
    levels = np.array([10, -10, 5, -5, 0])
    a = np.random.permutation(np.resize(levels, k // 512 * 4)).reshape(k // 512, 4)
    idx = np.arange(k)
    return np.exp2(a[idx // 512, idx % 128 // 32])


BF16 = ml_dtypes.bfloat16


def bf(x):
    return np.asarray(x, np.float32).astype(BF16)


def f64(x):
    return np.asarray(x).astype(np.float64)


E2M1 = np.array([0.0, 0.5, 1.0, 1.5, 2.0, 3.0, 4.0, 6.0, -0.0, -0.5, -1.0, -1.5, -2.0, -3.0, -4.0, -6.0])


def pack_weight(w, fmt):
    k, n = w.shape
    w = f64(bf(w)).reshape(k // 32, 32, n)
    amax = np.abs(w).max(1)
    if fmt == "e4m3":
        byte = np.frexp(amax)[1] - 1 + 127 - 7
    else:
        mant, ex = np.frexp(amax / 6.0)
        byte = np.where(mant > 0.5, ex, ex - 1) + 127
    byte = np.clip(np.where(amax > 0, byte, 1), 1, 254)
    scaled = (w * np.exp2(127.0 - byte)[:, None, :]).reshape(k, n).astype(np.float32)
    by_word = np.ascontiguousarray(scaled.reshape(k // 512, 128, 4, n).transpose(0, 1, 3, 2))
    if fmt == "e4m3":
        words = by_word.astype(ml_dtypes.float8_e4m3fn).view(np.uint8)
    else:
        c = by_word.astype(ml_dtypes.float4_e2m1fn).view(np.uint8) & 0xF
        words = c[..., 0::2] | (c[..., 1::2] << 4)
    return np.ascontiguousarray(words), np.ascontiguousarray(byte.astype(np.uint8).reshape(k // 512, 16, n))


def unpack_weight(words, scales, fmt):
    g, p, n, _ = words.shape
    if fmt == "e4m3":
        vals = np.ascontiguousarray(words).view(ml_dtypes.float8_e4m3fn).astype(np.float64)
    else:
        nib = np.empty((g, p, n, 4), np.uint8)
        nib[..., 0::2] = words & 0xF
        nib[..., 1::2] = words >> 4
        vals = E2M1[nib]
    vals = vals * np.repeat(np.exp2(scales.astype(np.float64) - 127.0), 8, axis=1)[..., None]
    return vals.transpose(0, 1, 3, 2).reshape(g * 512, n)


B, CIN, COUT, T, R, C = 2, 512, 512, 8, 8, 8


def setup_inputs():
    s = mx_kscale(CIN)
    x = np.random.standard_normal((B, CIN, T, R, C)) * s[None, :, None, None, None]
    W = np.random.standard_normal((7 * COUT, CIN)) * 0.5 / np.sqrt(CIN) / s[None, :]
    words, scales = pack_weight(np.ascontiguousarray(W.T), "e4m3")
    return {"x": bf(x), "W_words": words, "W_scales": scales}


def _shift(a, axis, d):
    pads = [(0, 0)] * a.ndim
    idx = [slice(None)] * a.ndim
    if d > 0:
        pads[axis] = (1, 0)
        idx[axis] = slice(0, -1)
    else:
        pads[axis] = (0, 1)
        idx[axis] = slice(1, None)
    return np.pad(a, pads)[tuple(idx)]


def reference(x, W_words, W_scales):
    cout = W_words.shape[2] // 7
    xq = mxq(f64(x), 1, "e4m3")
    Wq = unpack_weight(W_words, W_scales, "e4m3").T
    all_out = xq.transpose(0, 2, 3, 4, 1) @ Wq.T
    a = all_out.reshape(*all_out.shape[:4], 7, cout)
    out = a[..., 0, :]
    out = out + _shift(a[..., 1, :], 1, +1)
    out = out + _shift(a[..., 2, :], 1, -1)
    out = out + _shift(a[..., 3, :], 2, +1)
    out = out + _shift(a[..., 4, :], 2, -1)
    out = out + _shift(a[..., 5, :], 3, +1)
    out = out + _shift(a[..., 6, :], 3, -1)
    return np.transpose(out, (0, 4, 1, 2, 3))

@@ -1,0 +1,186 @@
+from contextlib import ExitStack
+
+import concourse.mybir as mybir
+
+FP8X4 = mybir.dt.float8_e4m3fn_x4
+BF16 = mybir.dt.bfloat16
+F32 = mybir.dt.float32
+I32 = mybir.dt.int32
+U8 = mybir.dt.uint8
+
+P = 128
+PACK = 4
+BATCH = 2
+CIN = P * PACK
+COUT = 512
+M_TILES = COUT // P
+DIRECTIONS = 7
+ROW = 8
+SLAB = 64
+VOX = 512
+
+FLOPS = 2 * BATCH * VOX * CIN * DIRECTIONS * COUT
+
+
+def kept_range(shift, length):
+    return max(0, -shift), length - max(0, shift)
+
+
+def tile_stackeddirectionalconv3d_kernel(tc, x, W_words, W_scales, out):
+    nc = tc.nc
+    with ExitStack() as ctx:
+        keep = ctx.enter_context(tc.tile_pool(name="keep", bufs=1))
+        results = ctx.enter_context(tc.tile_pool(name="results", bufs=BATCH * M_TILES))
+        banks = ctx.enter_context(tc.psum_pool(name="banks", bufs=BATCH * M_TILES))
+        ctx.enter_context(tc.manual_schedule())
+
+        w_words = keep.tile([P, DIRECTIONS * COUT], I32, align_bytes=64)
+        w_plane = keep.tile([P, DIRECTIONS * COUT], U8, align_bytes=64)
+        raw = keep.tile([P, BATCH, PACK, VOX], BF16)
+        centre_bf = keep.tile([P, BATCH, VOX, PACK], BF16, align_bytes=64)
+        centre_words = keep.tile([P, BATCH, SLAB + VOX + SLAB], I32, align_bytes=64)
+        centre_plane = keep.tile([P, BATCH, SLAB + VOX + SLAB], U8, align_bytes=64)
+        moved_bf = {}
+        moved_words = {}
+        moved_plane = {}
+        for shift in (-ROW, ROW, -1, 1):
+            label = "from_%s%d" % ("minus" if shift < 0 else "plus", abs(shift))
+            moved_words[shift] = keep.tile([P, BATCH, VOX], I32, align_bytes=64, name="words_" + label)
+            moved_plane[shift] = keep.tile([P, BATCH, VOX], U8, align_bytes=64, name="plane_" + label)
+        for shift in (-1, 1):
+            label = "from_%s%d" % ("minus" if shift < 0 else "plus", abs(shift))
+            moved_bf[shift] = keep.tile([P, VOX, PACK], BF16, align_bytes=64, name="bf_" + label)
+
+        def load_x(b):
+            nc.sync.dma_start(out=raw[:, b], in_=x[b].rearrange("(p j) t r c -> p j (t r c)", j=PACK))
+
+        def load_w_direction(d):
+            w_bytes = W_words[0].rearrange("p n j -> p (n j)")
+            nc.sync.dma_start(
+                out=w_words[:, d * COUT : (d + 1) * COUT],
+                in_=w_bytes[:, d * COUT * PACK : (d + 1) * COUT * PACK].bitcast(I32),
+            )
+
+        load_x(0)
+        nc.vector.memset(w_plane[:].bitcast(I32), 0)
+        for quadrant in range(4):
+            nc.sync.dma_start(
+                out=w_plane[32 * quadrant : 32 * quadrant + 4, :].bitcast(I32),
+                in_=W_scales[0, 4 * quadrant : 4 * quadrant + 4, :].bitcast(I32),
+            )
+        for d in (0, 1, 2):
+            load_w_direction(d)
+        load_x(1)
+        for d in (3, 4, 5, 6):
+            load_w_direction(d)
+
+        nc.vector.memset(centre_plane[:].bitcast(I32), 0)
+        nc.vector.memset(centre_words[:, :, 0:SLAB], 0)
+        nc.vector.memset(centre_words[:, :, SLAB + VOX :], 0)
+        for shift in (-ROW, ROW):
+            lo, hi = kept_range(shift, SLAB)
+            slabs = moved_words[shift][:].rearrange("p b (t s) -> p (b t) s", s=SLAB)
+            if lo > 0:
+                nc.vector.memset(slabs[:, :, 0:lo], 0)
+            else:
+                nc.vector.memset(slabs[:, :, hi:SLAB], 0)
+        for shift in (-1, 1):
+            nc.vector.memset(moved_bf[shift][:].rearrange("p v j -> p (v j)").bitcast(I32), 0)
+
+        def regroup_centre(b):
+            nc.vector.tensor_copy(
+                out=centre_bf[:, b].rearrange("p (g i) j -> p g j i", i=4),
+                in_=raw[:, b].rearrange("p j (g i) -> p g j i", i=4),
+            )
+
+        def quantise_centre(b):
+            nc.vector.quantize_mx(
+                out=centre_words[:, b, SLAB : SLAB + VOX].bitcast(FP8X4),
+                scales=centre_plane[:, b, SLAB : SLAB + VOX],
+                in_=centre_bf[:, b].rearrange("p v j -> p (v j)"),
+            )
+
+        def move_rows(b, shift):
+            lo, hi = kept_range(shift, SLAB)
+            source = centre_words[:, b, SLAB : SLAB + VOX].rearrange("p (t s) -> p t s", s=SLAB)
+            target = moved_words[shift][:, b].rearrange("p (t s) -> p t s", s=SLAB)
+            nc.vector.tensor_copy(out=target[:, :, lo:hi], in_=source[:, :, lo + shift : hi + shift])
+            nc.vector.tensor_copy(
+                out=moved_plane[shift][:, b].bitcast(I32),
+                in_=centre_plane[:, b, SLAB + shift : SLAB + shift + VOX].bitcast(I32),
+            )
+
+        def regroup_moved(b, shift):
+            lo, hi = kept_range(shift, ROW)
+            nc.scalar.copy(
+                out=moved_bf[shift][:].rearrange("p (s c) j -> p s j c", c=ROW)[:, :, :, lo:hi],
+                in_=raw[:, b].rearrange("p j (s c) -> p s j c", c=ROW)[:, :, :, lo + shift : hi + shift],
+            )
+
+        def quantise_moved(b, shift):
+            nc.vector.quantize_mx(
+                out=moved_words[shift][:, b].bitcast(FP8X4),
+                scales=moved_plane[shift][:, b],
+                in_=moved_bf[shift][:].rearrange("p v j -> p (v j)"),
+            )
+
+        reads_from = (0, -SLAB, SLAB, -ROW, ROW, -1, 1)
+
+        def mx_pass(acc, b, m, d):
+            shift = reads_from[d]
+            if abs(shift) in (0, SLAB):
+                window = slice(SLAB + shift, SLAB + shift + VOX)
+                x_words, x_plane = centre_words[:, b, window], centre_plane[:, b, window]
+            else:
+                x_words, x_plane = moved_words[shift][:, b], moved_plane[shift][:, b]
+            w_cols = slice(d * COUT + m * P, d * COUT + (m + 1) * P)
+            nc.tensor.matmul_mx(
+                out=acc[:],
+                lhsT=w_words[:, w_cols].bitcast(FP8X4),
+                lhsT_scale=w_plane[:, w_cols],
+                rhs=x_words.bitcast(FP8X4),
+                rhs_scale=x_plane,
+                start=(d == 0),
+                stop=(d == DIRECTIONS - 1),
+            )
+
+        def store(acc, b, m):
+            result = results.tile([P, VOX], F32, name="result")
+            if m % 2 == 0:
+                nc.scalar.copy(out=result[:], in_=acc[:])
+            else:
+                nc.vector.tensor_copy(out=result[:], in_=acc[:])
+            nc.sync.dma_start(
+                out=out[b, m * P : (m + 1) * P].rearrange("o t r c -> o (t r c)"), in_=result[:]
+            )
+
+        regroup_centre(0)
+        regroup_moved(0, -1)
+        regroup_moved(0, 1)
+        quantise_centre(0)
+        move_rows(0, -ROW)
+        move_rows(0, ROW)
+        regroup_centre(1)
+        quantise_moved(0, -1)
+        quantise_centre(1)
+        quantise_moved(0, 1)
+        accs = [banks.tile([P, VOX], F32, name="acc") for m in range(M_TILES)]
+        for d in range(DIRECTIONS):
+            for m in range(M_TILES):
+                mx_pass(accs[m], 0, m, d)
+
+        regroup_moved(1, -1)
+        regroup_moved(1, 1)
+        move_rows(1, -ROW)
+        move_rows(1, ROW)
+        quantise_moved(1, -1)
+        quantise_moved(1, 1)
+
+        for m in range(M_TILES):
+            store(accs[m], 0, m)
+
+        for m in range(M_TILES):
+            acc = banks.tile([P, VOX], F32, name="acc")
+            for d in range(DIRECTIONS):
+                mx_pass(acc, 1, m, d)
+            store(acc, 1, m)

@@ -18,6 +18,9 @@ DIRECTIONS = 7
 ROW = 8
 SLAB = 64
 VOX = 512
+HALVES = 2
+HALF = VOX // HALVES
+PSUM_BANKS = 8
 
 FLOPS = 2 * BATCH * VOX * CIN * DIRECTIONS * COUT
 
@@ -30,8 +33,8 @@ def tile_stackeddirectionalconv3d_kernel(tc, x, W_words, W_scales, out):
     nc = tc.nc
     with ExitStack() as ctx:
         keep = ctx.enter_context(tc.tile_pool(name="keep", bufs=1))
-        results = ctx.enter_context(tc.tile_pool(name="results", bufs=BATCH * M_TILES))
-        banks = ctx.enter_context(tc.psum_pool(name="banks", bufs=BATCH * M_TILES))
+        results = ctx.enter_context(tc.tile_pool(name="results", bufs=PSUM_BANKS))
+        banks = ctx.enter_context(tc.psum_pool(name="banks", bufs=PSUM_BANKS))
         ctx.enter_context(tc.manual_schedule())
 
         w_words = keep.tile([P, DIRECTIONS * COUT], I32, align_bytes=64)
@@ -87,17 +90,20 @@ def tile_stackeddirectionalconv3d_kernel(tc, x, W_words, W_scales, out):
         for shift in (-1, 1):
             nc.vector.memset(moved_bf[shift][:].rearrange("p v j -> p (v j)").bitcast(I32), 0)
 
-        def regroup_centre(b):
-            nc.vector.tensor_copy(
-                out=centre_bf[:, b].rearrange("p (g i) j -> p g j i", i=4),
-                in_=raw[:, b].rearrange("p j (g i) -> p g j i", i=4),
+        def regroup_centre(copy, b, h):
+            voxels = slice(h * HALF, (h + 1) * HALF)
+            copy(
+                out=centre_bf[:, b, voxels, :].rearrange("p (g i) j -> p g j i", i=4),
+                in_=raw[:, b, :, voxels].rearrange("p j (g i) -> p g j i", i=4),
             )
 
-        def quantise_centre(b):
+        def quantise_centre(b, h):
+            voxels = slice(h * HALF, (h + 1) * HALF)
+            columns = slice(SLAB + h * HALF, SLAB + (h + 1) * HALF)
             nc.vector.quantize_mx(
-                out=centre_words[:, b, SLAB : SLAB + VOX].bitcast(FP8X4),
-                scales=centre_plane[:, b, SLAB : SLAB + VOX],
-                in_=centre_bf[:, b].rearrange("p v j -> p (v j)"),
+                out=centre_words[:, b, columns].bitcast(FP8X4),
+                scales=centre_plane[:, b, columns],
+                in_=centre_bf[:, b, voxels, :].rearrange("p v j -> p (v j)"),
             )
 
         def move_rows(b, shift):
@@ -110,11 +116,13 @@ def tile_stackeddirectionalconv3d_kernel(tc, x, W_words, W_scales, out):
                 in_=centre_plane[:, b, SLAB + shift : SLAB + shift + VOX].bitcast(I32),
             )
 
-        def regroup_moved(b, shift):
+        def move_columns(copy, b, shift):
             lo, hi = kept_range(shift, ROW)
-            nc.scalar.copy(
-                out=moved_bf[shift][:].rearrange("p (s c) j -> p s j c", c=ROW)[:, :, :, lo:hi],
-                in_=raw[:, b].rearrange("p j (s c) -> p s j c", c=ROW)[:, :, :, lo + shift : hi + shift],
+            source = centre_bf[:, b].rearrange("p (s c) j -> p s (c j)", c=ROW)
+            target = moved_bf[shift][:].rearrange("p (s c) j -> p s (c j)", c=ROW)
+            copy(
+                out=target[:, :, lo * PACK : hi * PACK],
+                in_=source[:, :, (lo + shift) * PACK : (hi + shift) * PACK],
             )
 
         def quantise_moved(b, shift):
@@ -124,15 +132,28 @@ def tile_stackeddirectionalconv3d_kernel(tc, x, W_words, W_scales, out):
                 in_=moved_bf[shift][:].rearrange("p v j -> p (v j)"),
             )
 
+        def prepare(b):
+            regroup_centre(nc.vector.tensor_copy, b, 0)
+            regroup_centre(nc.scalar.copy, b, 1)
+            quantise_centre(b, 0)
+            quantise_centre(b, 1)
+            move_columns(nc.scalar.copy, b, -1)
+            move_rows(b, -ROW)
+            move_rows(b, ROW)
+            move_columns(nc.vector.tensor_copy, b, 1)
+            quantise_moved(b, -1)
+            quantise_moved(b, 1)
+
         reads_from = (0, -SLAB, SLAB, -ROW, ROW, -1, 1)
 
-        def mx_pass(acc, b, m, d):
+        def mx_pass(acc, b, m, h, d):
             shift = reads_from[d]
             if abs(shift) in (0, SLAB):
-                window = slice(SLAB + shift, SLAB + shift + VOX)
+                window = slice(SLAB + shift + h * HALF, SLAB + shift + (h + 1) * HALF)
                 x_words, x_plane = centre_words[:, b, window], centre_plane[:, b, window]
             else:
-                x_words, x_plane = moved_words[shift][:, b], moved_plane[shift][:, b]
+                window = slice(h * HALF, (h + 1) * HALF)
+                x_words, x_plane = moved_words[shift][:, b, window], moved_plane[shift][:, b, window]
             w_cols = slice(d * COUT + m * P, d * COUT + (m + 1) * P)
             nc.tensor.matmul_mx(
                 out=acc[:],
@@ -144,43 +165,29 @@ def tile_stackeddirectionalconv3d_kernel(tc, x, W_words, W_scales, out):
                 stop=(d == DIRECTIONS - 1),
             )
 
-        def store(acc, b, m):
-            result = results.tile([P, VOX], F32, name="result")
-            if m % 2 == 0:
-                nc.scalar.copy(out=result[:], in_=acc[:])
-            else:
-                nc.vector.tensor_copy(out=result[:], in_=acc[:])
-            nc.sync.dma_start(
-                out=out[b, m * P : (m + 1) * P].rearrange("o t r c -> o (t r c)"), in_=result[:]
-            )
+        def store(copy, acc, b, m, h):
+            result = results.tile([P, HALF], F32, name="result")
+            copy(out=result[:], in_=acc[:])
+            out_rows = out[b, m * P : (m + 1) * P].rearrange("o t r c -> o (t r c)")
+            nc.sync.dma_start(out=out_rows[:, h * HALF : (h + 1) * HALF], in_=result[:])
 
-        regroup_centre(0)
-        regroup_moved(0, -1)
-        regroup_moved(0, 1)
-        quantise_centre(0)
-        move_rows(0, -ROW)
-        move_rows(0, ROW)
-        regroup_centre(1)
-        quantise_moved(0, -1)
-        quantise_centre(1)
-        quantise_moved(0, 1)
-        accs = [banks.tile([P, VOX], F32, name="acc") for m in range(M_TILES)]
-        for d in range(DIRECTIONS):
-            for m in range(M_TILES):
-                mx_pass(accs[m], 0, m, d)
+        pieces = [(h, m) for h in range(HALVES) for m in range(M_TILES)]
 
-        regroup_moved(1, -1)
-        regroup_moved(1, 1)
-        move_rows(1, -ROW)
-        move_rows(1, ROW)
-        quantise_moved(1, -1)
-        quantise_moved(1, 1)
+        prepare(0)
+        accs = {}
+        for h, m in pieces:
+            accs[(h, m)] = banks.tile([P, HALF], F32, name="acc")
+        for d in range(DIRECTIONS - 2):
+            for h, m in pieces:
+                mx_pass(accs[(h, m)], 0, m, h, d)
+        prepare(1)
+        for h, m in pieces:
+            for d in range(DIRECTIONS - 2, DIRECTIONS):
+                mx_pass(accs[(h, m)], 0, m, h, d)
+            store(nc.scalar.copy, accs[(h, m)], 0, m, h)
 
-        for m in range(M_TILES):
-            store(accs[m], 0, m)
-
-        for m in range(M_TILES):
-            acc = banks.tile([P, VOX], F32, name="acc")
+        for h, m in pieces:
+            acc = banks.tile([P, HALF], F32, name="acc")
             for d in range(DIRECTIONS):
-                mx_pass(acc, 1, m, d)
-            store(acc, 1, m)
+                mx_pass(acc, 1, m, h, d)
+            store(nc.scalar.copy if m % 2 == 0 else nc.vector.tensor_copy, acc, 1, m, h)

@@ -21,6 +21,10 @@ VOX = 512
 HALVES = 2
 HALF = VOX // HALVES
 PSUM_BANKS = 8
+W_BLOCKS = DIRECTIONS * M_TILES
+PLANES = 4
+BLOCKS_PER_PLANE = W_BLOCKS // PLANES
+WARM_PASSES = 10
 
 FLOPS = 2 * BATCH * VOX * CIN * DIRECTIONS * COUT
 
@@ -38,7 +42,8 @@ def tile_stackeddirectionalconv3d_kernel(tc, x, W_words, W_scales, out):
         ctx.enter_context(tc.manual_schedule())
 
         w_words = keep.tile([P, DIRECTIONS * COUT], I32, align_bytes=64)
-        w_plane = keep.tile([P, DIRECTIONS * COUT], U8, align_bytes=64)
+        w_planes = keep.tile([P, BLOCKS_PER_PLANE * P], U8, align_bytes=64)
+        zeros = keep.tile([P, VOX], BF16)
         raw = keep.tile([P, BATCH, PACK, VOX], BF16)
         centre_bf = keep.tile([P, BATCH, VOX, PACK], BF16, align_bytes=64)
         centre_words = keep.tile([P, BATCH, SLAB + VOX + SLAB], I32, align_bytes=64)
@@ -64,18 +69,24 @@ def tile_stackeddirectionalconv3d_kernel(tc, x, W_words, W_scales, out):
                 in_=w_bytes[:, d * COUT * PACK : (d + 1) * COUT * PACK].bitcast(I32),
             )
 
-        load_x(0)
-        nc.vector.memset(w_plane[:].bitcast(I32), 0)
+        nc.vector.memset(w_planes[:].bitcast(I32), 0)
         for quadrant in range(4):
+            scale_rows = W_scales[0, 4 * quadrant : 4 * quadrant + 4, :]
             nc.sync.dma_start(
-                out=w_plane[32 * quadrant : 32 * quadrant + 4, :].bitcast(I32),
-                in_=W_scales[0, 4 * quadrant : 4 * quadrant + 4, :].bitcast(I32),
+                out=w_planes[32 * quadrant : 32 * quadrant + 4 * PLANES, :].bitcast(I32),
+                in_=scale_rows.rearrange("r (k n) -> k r n", k=PLANES).bitcast(I32),
             )
+        load_x(0)
         for d in (0, 1, 2):
             load_w_direction(d)
         load_x(1)
         for d in (3, 4, 5, 6):
             load_w_direction(d)
+
+        nc.vector.memset(zeros[:].bitcast(I32), 0)
+        warm = banks.tile([P, VOX], F32, name="acc")
+        for i in range(WARM_PASSES):
+            nc.tensor.matmul(out=warm[:], lhsT=zeros[:, 0:P], rhs=zeros[:], start=True, stop=True)
 
         nc.vector.memset(centre_plane[:].bitcast(I32), 0)
         nc.vector.memset(centre_words[:, :, 0:SLAB], 0)
@@ -154,11 +165,12 @@ def tile_stackeddirectionalconv3d_kernel(tc, x, W_words, W_scales, out):
             else:
                 window = slice(h * HALF, (h + 1) * HALF)
                 x_words, x_plane = moved_words[shift][:, b, window], moved_plane[shift][:, b, window]
-            w_cols = slice(d * COUT + m * P, d * COUT + (m + 1) * P)
+            block = d * M_TILES + m
+            k, place = divmod(block, BLOCKS_PER_PLANE)
             nc.tensor.matmul_mx(
                 out=acc[:],
-                lhsT=w_words[:, w_cols].bitcast(FP8X4),
-                lhsT_scale=w_plane[:, w_cols],
+                lhsT=w_words[:, block * P : (block + 1) * P].bitcast(FP8X4),
+                lhsT_scale=w_planes[4 * k : P, place * P : (place + 1) * P],
                 rhs=x_words.bitcast(FP8X4),
                 rhs_scale=x_plane,
                 start=(d == 0),

@@ -69,6 +69,13 @@ def tile_stackeddirectionalconv3d_kernel(tc, x, W_words, W_scales, out):
                 in_=w_bytes[:, d * COUT * PACK : (d + 1) * COUT * PACK].bitcast(I32),
             )
 
+        load_x(0)
+
+        nc.vector.memset(zeros[:].bitcast(I32), 0)
+        warm = banks.tile([P, VOX], F32, name="acc")
+        for i in range(WARM_PASSES):
+            nc.tensor.matmul(out=warm[:], lhsT=zeros[:, 0:P], rhs=zeros[:], start=True, stop=True)
+
         nc.vector.memset(w_planes[:].bitcast(I32), 0)
         for quadrant in range(4):
             scale_rows = W_scales[0, 4 * quadrant : 4 * quadrant + 4, :]
@@ -76,17 +83,11 @@ def tile_stackeddirectionalconv3d_kernel(tc, x, W_words, W_scales, out):
                 out=w_planes[32 * quadrant : 32 * quadrant + 4 * PLANES, :].bitcast(I32),
                 in_=scale_rows.rearrange("r (k n) -> k r n", k=PLANES).bitcast(I32),
             )
-        load_x(0)
-        for d in (0, 1, 2):
+        for d in (0, 1, 2, 3):
             load_w_direction(d)
         load_x(1)
-        for d in (3, 4, 5, 6):
+        for d in (4, 5, 6):
             load_w_direction(d)
-
-        nc.vector.memset(zeros[:].bitcast(I32), 0)
-        warm = banks.tile([P, VOX], F32, name="acc")
-        for i in range(WARM_PASSES):
-            nc.tensor.matmul(out=warm[:], lhsT=zeros[:, 0:P], rhs=zeros[:], start=True, stop=True)
 
         nc.vector.memset(centre_plane[:].bitcast(I32), 0)
         nc.vector.memset(centre_words[:, :, 0:SLAB], 0)

@@ -158,49 +158,55 @@ def tile_stackeddirectionalconv3d_kernel(tc, x, W_words, W_scales, out):
 
         reads_from = (0, -SLAB, SLAB, -ROW, ROW, -1, 1)
 
-        def mx_pass(acc, b, m, h, d):
+        def mx_pass(acc_columns, b, m, d, first, width, start):
             shift = reads_from[d]
             if abs(shift) in (0, SLAB):
-                window = slice(SLAB + shift + h * HALF, SLAB + shift + (h + 1) * HALF)
+                window = slice(SLAB + shift + first, SLAB + shift + first + width)
                 x_words, x_plane = centre_words[:, b, window], centre_plane[:, b, window]
             else:
-                window = slice(h * HALF, (h + 1) * HALF)
+                window = slice(first, first + width)
                 x_words, x_plane = moved_words[shift][:, b, window], moved_plane[shift][:, b, window]
             block = d * M_TILES + m
             k, place = divmod(block, BLOCKS_PER_PLANE)
             nc.tensor.matmul_mx(
-                out=acc[:],
+                out=acc_columns,
                 lhsT=w_words[:, block * P : (block + 1) * P].bitcast(FP8X4),
                 lhsT_scale=w_planes[4 * k : P, place * P : (place + 1) * P],
                 rhs=x_words.bitcast(FP8X4),
                 rhs_scale=x_plane,
-                start=(d == 0),
+                start=start,
                 stop=(d == DIRECTIONS - 1),
             )
 
-        def store(copy, acc, b, m, h):
-            result = results.tile([P, HALF], F32, name="result")
+        def store(copy, acc, b, m, first, width):
+            result = results.tile([P, width], F32, name="result")
             copy(out=result[:], in_=acc[:])
             out_rows = out[b, m * P : (m + 1) * P].rearrange("o t r c -> o (t r c)")
-            nc.sync.dma_start(out=out_rows[:, h * HALF : (h + 1) * HALF], in_=result[:])
-
-        pieces = [(h, m) for h in range(HALVES) for m in range(M_TILES)]
+            nc.sync.dma_start(out=out_rows[:, first : first + width], in_=result[:])
 
         prepare(0)
-        accs = {}
-        for h, m in pieces:
-            accs[(h, m)] = banks.tile([P, HALF], F32, name="acc")
-        for d in range(DIRECTIONS - 2):
-            for h, m in pieces:
-                mx_pass(accs[(h, m)], 0, m, h, d)
+        accs = []
+        for m in range(M_TILES):
+            accs.append(banks.tile([P, VOX], F32, name="acc"))
+        for h in range(HALVES):
+            for m in range(M_TILES):
+                mx_pass(accs[m][:, h * HALF : (h + 1) * HALF], 0, m, 0, h * HALF, HALF, h == 0)
+        for d in range(1, DIRECTIONS - 2):
+            for m in range(M_TILES):
+                mx_pass(accs[m][:], 0, m, d, 0, VOX, False)
         prepare(1)
-        for h, m in pieces:
+        for m in range(M_TILES):
             for d in range(DIRECTIONS - 2, DIRECTIONS):
-                mx_pass(accs[(h, m)], 0, m, h, d)
-            store(nc.scalar.copy, accs[(h, m)], 0, m, h)
+                mx_pass(accs[m][:], 0, m, d, 0, VOX, False)
+            store(nc.scalar.copy, accs[m], 0, m, 0, VOX)
 
-        for h, m in pieces:
+        for m in range(M_TILES - 1):
+            acc = banks.tile([P, VOX], F32, name="acc")
+            for d in range(DIRECTIONS):
+                mx_pass(acc[:], 1, m, d, 0, VOX, d == 0)
+            store(nc.scalar.copy if m % 2 == 0 else nc.vector.tensor_copy, acc, 1, m, 0, VOX)
+        for h in range(HALVES):
             acc = banks.tile([P, HALF], F32, name="acc")
             for d in range(DIRECTIONS):
-                mx_pass(acc, 1, m, h, d)
-            store(nc.scalar.copy if m % 2 == 0 else nc.vector.tensor_copy, acc, 1, m, h)
+                mx_pass(acc[:], 1, M_TILES - 1, d, h * HALF, HALF, d == 0)
+            store(nc.scalar.copy if h == 0 else nc.vector.tensor_copy, acc, 1, M_TILES - 1, h * HALF, HALF)

@@ -24,7 +24,7 @@ PSUM_BANKS = 8
 W_BLOCKS = DIRECTIONS * M_TILES
 PLANES = 4
 BLOCKS_PER_PLANE = W_BLOCKS // PLANES
-WARM_PASSES = 10
+WARM_PASSES = 7
 
 FLOPS = 2 * BATCH * VOX * CIN * DIRECTIONS * COUT
 

@@ -62,12 +62,15 @@ def tile_stackeddirectionalconv3d_kernel(tc, x, W_words, W_scales, out):
         def load_x(b):
             nc.sync.dma_start(out=raw[:, b], in_=x[b].rearrange("(p j) t r c -> p j (t r c)", j=PACK))
 
-        def load_w_direction(d):
+        def load_w_columns(first, width):
             w_bytes = W_words[0].rearrange("p n j -> p (n j)")
             nc.sync.dma_start(
-                out=w_words[:, d * COUT : (d + 1) * COUT],
-                in_=w_bytes[:, d * COUT * PACK : (d + 1) * COUT * PACK].bitcast(I32),
+                out=w_words[:, first : first + width],
+                in_=w_bytes[:, first * PACK : (first + width) * PACK].bitcast(I32),
             )
+
+        def load_w_direction(d):
+            load_w_columns(d * COUT, COUT)
 
         load_x(0)
 
@@ -83,7 +86,9 @@ def tile_stackeddirectionalconv3d_kernel(tc, x, W_words, W_scales, out):
                 out=w_planes[32 * quadrant : 32 * quadrant + 4 * PLANES, :].bitcast(I32),
                 in_=scale_rows.rearrange("r (k n) -> k r n", k=PLANES).bitcast(I32),
             )
-        for d in (0, 1, 2, 3):
+        load_w_columns(0, COUT // 2)
+        load_w_columns(COUT // 2, COUT // 2)
+        for d in (1, 2, 3):
             load_w_direction(d)
         load_x(1)
         for d in (4, 5, 6):
@@ -102,16 +107,16 @@ def tile_stackeddirectionalconv3d_kernel(tc, x, W_words, W_scales, out):
         for shift in (-1, 1):
             nc.vector.memset(moved_bf[shift][:].rearrange("p v j -> p (v j)").bitcast(I32), 0)
 
-        def regroup_centre(copy, b, h):
-            voxels = slice(h * HALF, (h + 1) * HALF)
+        def regroup_centre(copy, b, first, width):
+            voxels = slice(first, first + width)
             copy(
                 out=centre_bf[:, b, voxels, :].rearrange("p (g i) j -> p g j i", i=4),
                 in_=raw[:, b, :, voxels].rearrange("p j (g i) -> p g j i", i=4),
             )
 
-        def quantise_centre(b, h):
-            voxels = slice(h * HALF, (h + 1) * HALF)
-            columns = slice(SLAB + h * HALF, SLAB + (h + 1) * HALF)
+        def quantise_centre(b, first, width):
+            voxels = slice(first, first + width)
+            columns = slice(SLAB + first, SLAB + first + width)
             nc.vector.quantize_mx(
                 out=centre_words[:, b, columns].bitcast(FP8X4),
                 scales=centre_plane[:, b, columns],
@@ -144,11 +149,14 @@ def tile_stackeddirectionalconv3d_kernel(tc, x, W_words, W_scales, out):
                 in_=moved_bf[shift][:].rearrange("p v j -> p (v j)"),
             )
 
-        def prepare(b):
-            regroup_centre(nc.vector.tensor_copy, b, 0)
-            regroup_centre(nc.scalar.copy, b, 1)
-            quantise_centre(b, 0)
-            quantise_centre(b, 1)
+        def prepare(b, pieces_of_first_half):
+            piece = HALF // pieces_of_first_half
+            for i in range(pieces_of_first_half):
+                regroup_centre(nc.vector.tensor_copy, b, i * piece, piece)
+            regroup_centre(nc.scalar.copy, b, HALF, HALF)
+            for i in range(pieces_of_first_half):
+                quantise_centre(b, i * piece, piece)
+            quantise_centre(b, HALF, HALF)
             move_columns(nc.scalar.copy, b, -1)
             move_rows(b, -ROW)
             move_rows(b, ROW)
@@ -184,17 +192,17 @@ def tile_stackeddirectionalconv3d_kernel(tc, x, W_words, W_scales, out):
             out_rows = out[b, m * P : (m + 1) * P].rearrange("o t r c -> o (t r c)")
             nc.sync.dma_start(out=out_rows[:, first : first + width], in_=result[:])
 
-        prepare(0)
+        prepare(0, 2)
         accs = []
         for m in range(M_TILES):
             accs.append(banks.tile([P, VOX], F32, name="acc"))
-        for h in range(HALVES):
+        for first, width in ((0, HALF // 2), (HALF // 2, HALF // 2), (HALF, HALF)):
             for m in range(M_TILES):
-                mx_pass(accs[m][:, h * HALF : (h + 1) * HALF], 0, m, 0, h * HALF, HALF, h == 0)
+                mx_pass(accs[m][:, first : first + width], 0, m, 0, first, width, first == 0)
         for d in range(1, DIRECTIONS - 2):
             for m in range(M_TILES):
                 mx_pass(accs[m][:], 0, m, d, 0, VOX, False)
-        prepare(1)
+        prepare(1, 1)
         for m in range(M_TILES):
             for d in range(DIRECTIONS - 2, DIRECTIONS):
                 mx_pass(accs[m][:], 0, m, d, 0, VOX, False)

@@ -208,11 +208,16 @@ def tile_stackeddirectionalconv3d_kernel(tc, x, W_words, W_scales, out):
                 mx_pass(accs[m][:], 0, m, d, 0, VOX, False)
             store(nc.scalar.copy, accs[m], 0, m, 0, VOX)
 
+        accs = []
         for m in range(M_TILES - 1):
-            acc = banks.tile([P, VOX], F32, name="acc")
-            for d in range(DIRECTIONS):
-                mx_pass(acc[:], 1, m, d, 0, VOX, d == 0)
-            store(nc.scalar.copy if m % 2 == 0 else nc.vector.tensor_copy, acc, 1, m, 0, VOX)
+            accs.append(banks.tile([P, VOX], F32, name="acc"))
+        for d in range(DIRECTIONS - 2):
+            for m in range(M_TILES - 1):
+                mx_pass(accs[m][:], 1, m, d, 0, VOX, d == 0)
+        for m in range(M_TILES - 1):
+            for d in range(DIRECTIONS - 2, DIRECTIONS):
+                mx_pass(accs[m][:], 1, m, d, 0, VOX, False)
+            store(nc.scalar.copy if m % 2 == 0 else nc.vector.tensor_copy, accs[m], 1, m, 0, VOX)
         for h in range(HALVES):
             acc = banks.tile([P, HALF], F32, name="acc")
             for d in range(DIRECTIONS):

@@ -24,6 +24,9 @@ PSUM_BANKS = 8
 W_BLOCKS = DIRECTIONS * M_TILES
 PLANES = 4
 BLOCKS_PER_PLANE = W_BLOCKS // PLANES
+EARLY_BLOCKS = 3 * M_TILES
+EARLY_PER_PLANE = EARLY_BLOCKS // PLANES
+LATE_PER_PLANE = BLOCKS_PER_PLANE - EARLY_PER_PLANE
 WARM_PASSES = 7
 
 FLOPS = 2 * BATCH * VOX * CIN * DIRECTIONS * COUT
@@ -72,6 +75,24 @@ def tile_stackeddirectionalconv3d_kernel(tc, x, W_words, W_scales, out):
         def load_w_direction(d):
             load_w_columns(d * COUT, COUT)
 
+        def load_planes(first_block, per_plane, first_place):
+            for quadrant in range(4):
+                scale_rows = W_scales[
+                    0, 4 * quadrant : 4 * quadrant + 4, first_block * P : (first_block + PLANES * per_plane) * P
+                ]
+                nc.sync.dma_start(
+                    out=w_planes[
+                        32 * quadrant : 32 * quadrant + 4 * PLANES, first_place * P : (first_place + per_plane) * P
+                    ].bitcast(I32),
+                    in_=scale_rows.rearrange("r (k n) -> k r n", k=PLANES).bitcast(I32),
+                )
+
+        def plane_of(block):
+            if block < EARLY_BLOCKS:
+                return divmod(block, EARLY_PER_PLANE)
+            k, place = divmod(block - EARLY_BLOCKS, LATE_PER_PLANE)
+            return k, EARLY_PER_PLANE + place
+
         load_x(0)
 
         nc.vector.memset(zeros[:].bitcast(I32), 0)
@@ -80,19 +101,15 @@ def tile_stackeddirectionalconv3d_kernel(tc, x, W_words, W_scales, out):
             nc.tensor.matmul(out=warm[:], lhsT=zeros[:, 0:P], rhs=zeros[:], start=True, stop=True)
 
         nc.vector.memset(w_planes[:].bitcast(I32), 0)
-        for quadrant in range(4):
-            scale_rows = W_scales[0, 4 * quadrant : 4 * quadrant + 4, :]
-            nc.sync.dma_start(
-                out=w_planes[32 * quadrant : 32 * quadrant + 4 * PLANES, :].bitcast(I32),
-                in_=scale_rows.rearrange("r (k n) -> k r n", k=PLANES).bitcast(I32),
-            )
+        load_planes(0, EARLY_PER_PLANE, 0)
         load_w_columns(0, COUT // 2)
         load_w_columns(COUT // 2, COUT // 2)
-        for d in (1, 2, 3):
+        for d in (1, 2):
+            load_w_direction(d)
+        load_planes(EARLY_BLOCKS, LATE_PER_PLANE, EARLY_PER_PLANE)
+        for d in (3, 4, 5, 6):
             load_w_direction(d)
         load_x(1)
-        for d in (4, 5, 6):
-            load_w_direction(d)
 
         nc.vector.memset(centre_plane[:].bitcast(I32), 0)
         nc.vector.memset(centre_words[:, :, 0:SLAB], 0)
@@ -149,14 +166,13 @@ def tile_stackeddirectionalconv3d_kernel(tc, x, W_words, W_scales, out):
                 in_=moved_bf[shift][:].rearrange("p v j -> p (v j)"),
             )
 
-        def prepare(b, pieces_of_first_half):
-            piece = HALF // pieces_of_first_half
-            for i in range(pieces_of_first_half):
-                regroup_centre(nc.vector.tensor_copy, b, i * piece, piece)
-            regroup_centre(nc.scalar.copy, b, HALF, HALF)
-            for i in range(pieces_of_first_half):
-                quantise_centre(b, i * piece, piece)
-            quantise_centre(b, HALF, HALF)
+        def prepare(b, piece):
+            for first in range(0, HALF, piece):
+                regroup_centre(nc.vector.tensor_copy, b, first, piece)
+            for first in range(HALF, VOX, piece):
+                regroup_centre(nc.scalar.copy, b, first, piece)
+            for first in range(0, VOX, piece):
+                quantise_centre(b, first, piece)
             move_columns(nc.scalar.copy, b, -1)
             move_rows(b, -ROW)
             move_rows(b, ROW)
@@ -175,7 +191,7 @@ def tile_stackeddirectionalconv3d_kernel(tc, x, W_words, W_scales, out):
                 window = slice(first, first + width)
                 x_words, x_plane = moved_words[shift][:, b, window], moved_plane[shift][:, b, window]
             block = d * M_TILES + m
-            k, place = divmod(block, BLOCKS_PER_PLANE)
+            k, place = plane_of(block)
             nc.tensor.matmul_mx(
                 out=acc_columns,
                 lhsT=w_words[:, block * P : (block + 1) * P].bitcast(FP8X4),
@@ -192,17 +208,20 @@ def tile_stackeddirectionalconv3d_kernel(tc, x, W_words, W_scales, out):
             out_rows = out[b, m * P : (m + 1) * P].rearrange("o t r c -> o (t r c)")
             nc.sync.dma_start(out=out_rows[:, first : first + width], in_=result[:])
 
-        prepare(0, 2)
+        def first_direction(b, tiles, piece):
+            for first in range(0, VOX, piece):
+                for m in range(tiles):
+                    mx_pass(accs[m][:, first : first + piece], b, m, 0, first, piece, first == 0)
+
+        prepare(0, HALF // 2)
         accs = []
         for m in range(M_TILES):
             accs.append(banks.tile([P, VOX], F32, name="acc"))
-        for first, width in ((0, HALF // 2), (HALF // 2, HALF // 2), (HALF, HALF)):
-            for m in range(M_TILES):
-                mx_pass(accs[m][:, first : first + width], 0, m, 0, first, width, first == 0)
+        first_direction(0, M_TILES, HALF // 2)
         for d in range(1, DIRECTIONS - 2):
             for m in range(M_TILES):
                 mx_pass(accs[m][:], 0, m, d, 0, VOX, False)
-        prepare(1, 1)
+        prepare(1, HALF)
         for m in range(M_TILES):
             for d in range(DIRECTIONS - 2, DIRECTIONS):
                 mx_pass(accs[m][:], 0, m, d, 0, VOX, False)
@@ -211,9 +230,10 @@ def tile_stackeddirectionalconv3d_kernel(tc, x, W_words, W_scales, out):
         accs = []
         for m in range(M_TILES - 1):
             accs.append(banks.tile([P, VOX], F32, name="acc"))
-        for d in range(DIRECTIONS - 2):
+        first_direction(1, M_TILES - 1, HALF)
+        for d in range(1, DIRECTIONS - 2):
             for m in range(M_TILES - 1):
-                mx_pass(accs[m][:], 1, m, d, 0, VOX, d == 0)
+                mx_pass(accs[m][:], 1, m, d, 0, VOX, False)
         for m in range(M_TILES - 1):
             for d in range(DIRECTIONS - 2, DIRECTIONS):
                 mx_pass(accs[m][:], 1, m, d, 0, VOX, False)

@@ -44,23 +44,23 @@ def tile_stackeddirectionalconv3d_kernel(tc, x, W_words, W_scales, out):
         banks = ctx.enter_context(tc.psum_pool(name="banks", bufs=PSUM_BANKS))
         ctx.enter_context(tc.manual_schedule())
 
-        w_words = keep.tile([P, DIRECTIONS * COUT], I32, align_bytes=64)
-        w_planes = keep.tile([P, BLOCKS_PER_PLANE * P], U8, align_bytes=64)
+        w_words = keep.tile([P, DIRECTIONS * COUT], I32, align_bytes=256)
+        w_planes = keep.tile([P, BLOCKS_PER_PLANE * P], U8, align_bytes=256)
         zeros = keep.tile([P, VOX], BF16)
         raw = keep.tile([P, BATCH, PACK, VOX], BF16)
-        centre_bf = keep.tile([P, BATCH, VOX, PACK], BF16, align_bytes=64)
-        centre_words = keep.tile([P, BATCH, SLAB + VOX + SLAB], I32, align_bytes=64)
-        centre_plane = keep.tile([P, BATCH, SLAB + VOX + SLAB], U8, align_bytes=64)
+        centre_bf = keep.tile([P, BATCH, VOX, PACK], BF16, align_bytes=256)
+        centre_words = keep.tile([P, BATCH, SLAB + VOX + SLAB], I32, align_bytes=256)
+        centre_plane = keep.tile([P, BATCH, SLAB + VOX + SLAB], U8, align_bytes=256)
         moved_bf = {}
         moved_words = {}
         moved_plane = {}
         for shift in (-ROW, ROW, -1, 1):
             label = "from_%s%d" % ("minus" if shift < 0 else "plus", abs(shift))
-            moved_words[shift] = keep.tile([P, BATCH, VOX], I32, align_bytes=64, name="words_" + label)
-            moved_plane[shift] = keep.tile([P, BATCH, VOX], U8, align_bytes=64, name="plane_" + label)
+            moved_words[shift] = keep.tile([P, BATCH, VOX], I32, align_bytes=256, name="words_" + label)
+            moved_plane[shift] = keep.tile([P, BATCH, VOX], U8, align_bytes=256, name="plane_" + label)
         for shift in (-1, 1):
             label = "from_%s%d" % ("minus" if shift < 0 else "plus", abs(shift))
-            moved_bf[shift] = keep.tile([P, VOX, PACK], BF16, align_bytes=64, name="bf_" + label)
+            moved_bf[shift] = keep.tile([P, VOX, PACK], BF16, align_bytes=256, name="bf_" + label)
 
         def load_x(b):
             nc.sync.dma_start(out=raw[:, b], in_=x[b].rearrange("(p j) t r c -> p j (t r c)", j=PACK))

@@ -47,7 +47,7 @@ def tile_stackeddirectionalconv3d_kernel(tc, x, W_words, W_scales, out):
         w_words = keep.tile([P, DIRECTIONS * COUT], I32, align_bytes=256)
         w_planes = keep.tile([P, BLOCKS_PER_PLANE * P], U8, align_bytes=256)
         zeros = keep.tile([P, VOX], BF16)
-        raw = keep.tile([P, BATCH, PACK, VOX], BF16)
+        raw = keep.tile([P, BATCH, PACK, VOX], BF16, align_bytes=256)
         centre_bf = keep.tile([P, BATCH, VOX, PACK], BF16, align_bytes=256)
         centre_words = keep.tile([P, BATCH, SLAB + VOX + SLAB], I32, align_bytes=256)
         centre_plane = keep.tile([P, BATCH, SLAB + VOX + SLAB], U8, align_bytes=256)
@@ -203,7 +203,7 @@ def tile_stackeddirectionalconv3d_kernel(tc, x, W_words, W_scales, out):
             )
 
         def store(copy, acc, b, m, first, width):
-            result = results.tile([P, width], F32, name="result")
+            result = results.tile([P, width], F32, name="result", align_bytes=256)
             copy(out=result[:], in_=acc[:])
             out_rows = out[b, m * P : (m + 1) * P].rearrange("o t r c -> o (t r c)")
             nc.sync.dma_start(out=out_rows[:, first : first + width], in_=result[:])
@@ -238,8 +238,9 @@ def tile_stackeddirectionalconv3d_kernel(tc, x, W_words, W_scales, out):
             for d in range(DIRECTIONS - 2, DIRECTIONS):
                 mx_pass(accs[m][:], 1, m, d, 0, VOX, False)
             store(nc.scalar.copy if m % 2 == 0 else nc.vector.tensor_copy, accs[m], 1, m, 0, VOX)
-        for h in range(HALVES):
-            acc = banks.tile([P, HALF], F32, name="acc")
+        for first, width in ((0, HALF), (HALF, HALF // 2), (HALF + HALF // 2, HALF // 2)):
+            acc = banks.tile([P, width], F32, name="acc")
             for d in range(DIRECTIONS):
-                mx_pass(acc[:], 1, M_TILES - 1, d, h * HALF, HALF, d == 0)
-            store(nc.scalar.copy if h == 0 else nc.vector.tensor_copy, acc, 1, M_TILES - 1, h * HALF, HALF)
+                mx_pass(acc[:], 1, M_TILES - 1, d, first, width, d == 0)
+            last = first + width == VOX
+            store(nc.vector.tensor_copy if last else nc.scalar.copy, acc, 1, M_TILES - 1, first, width)

from contextlib import ExitStack

import concourse.mybir as mybir

FP8X4 = mybir.dt.float8_e4m3fn_x4
BF16 = mybir.dt.bfloat16
F32 = mybir.dt.float32
I32 = mybir.dt.int32
U8 = mybir.dt.uint8

P = 128
PACK = 4
BATCH = 2
CIN = P * PACK
COUT = 512
M_TILES = COUT // P
DIRECTIONS = 7
ROW = 8
SLAB = 64
VOX = 512
HALVES = 2
HALF = VOX // HALVES
PSUM_BANKS = 8
W_BLOCKS = DIRECTIONS * M_TILES
PLANES = 4
BLOCKS_PER_PLANE = W_BLOCKS // PLANES
EARLY_BLOCKS = 3 * M_TILES
EARLY_PER_PLANE = EARLY_BLOCKS // PLANES
LATE_PER_PLANE = BLOCKS_PER_PLANE - EARLY_PER_PLANE
WARM_PASSES = 7

FLOPS = 2 * BATCH * VOX * CIN * DIRECTIONS * COUT


def kept_range(shift, length):
    return max(0, -shift), length - max(0, shift)


def tile_stackeddirectionalconv3d_kernel(tc, x, W_words, W_scales, out):
    nc = tc.nc
    with ExitStack() as ctx:
        keep = ctx.enter_context(tc.tile_pool(name="keep", bufs=1))
        results = ctx.enter_context(tc.tile_pool(name="results", bufs=PSUM_BANKS))
        banks = ctx.enter_context(tc.psum_pool(name="banks", bufs=PSUM_BANKS))
        ctx.enter_context(tc.manual_schedule())

        w_words = keep.tile([P, DIRECTIONS * COUT], I32, align_bytes=256)
        w_planes = keep.tile([P, BLOCKS_PER_PLANE * P], U8, align_bytes=256)
        zeros = keep.tile([P, VOX], BF16)
        raw = keep.tile([P, BATCH, PACK, VOX], BF16, align_bytes=256)
        centre_bf = keep.tile([P, BATCH, VOX, PACK], BF16, align_bytes=256)
        centre_words = keep.tile([P, BATCH, SLAB + VOX + SLAB], I32, align_bytes=256)
        centre_plane = keep.tile([P, BATCH, SLAB + VOX + SLAB], U8, align_bytes=256)
        moved_bf = {}
        moved_words = {}
        moved_plane = {}
        for shift in (-ROW, ROW, -1, 1):
            label = "from_%s%d" % ("minus" if shift < 0 else "plus", abs(shift))
            moved_words[shift] = keep.tile([P, BATCH, VOX], I32, align_bytes=256, name="words_" + label)
            moved_plane[shift] = keep.tile([P, BATCH, VOX], U8, align_bytes=256, name="plane_" + label)
        for shift in (-1, 1):
            label = "from_%s%d" % ("minus" if shift < 0 else "plus", abs(shift))
            moved_bf[shift] = keep.tile([P, VOX, PACK], BF16, align_bytes=256, name="bf_" + label)

        def load_x(b):
            nc.sync.dma_start(out=raw[:, b], in_=x[b].rearrange("(p j) t r c -> p j (t r c)", j=PACK))

        def load_w_columns(first, width):
            w_bytes = W_words[0].rearrange("p n j -> p (n j)")
            nc.sync.dma_start(
                out=w_words[:, first : first + width],
                in_=w_bytes[:, first * PACK : (first + width) * PACK].bitcast(I32),
            )

        def load_w_direction(d):
            load_w_columns(d * COUT, COUT)

        def load_planes(first_block, per_plane, first_place):
            for quadrant in range(4):
                scale_rows = W_scales[
                    0, 4 * quadrant : 4 * quadrant + 4, first_block * P : (first_block + PLANES * per_plane) * P
                ]
                nc.sync.dma_start(
                    out=w_planes[
                        32 * quadrant : 32 * quadrant + 4 * PLANES, first_place * P : (first_place + per_plane) * P
                    ].bitcast(I32),
                    in_=scale_rows.rearrange("r (k n) -> k r n", k=PLANES).bitcast(I32),
                )

        def plane_of(block):
            if block < EARLY_BLOCKS:
                return divmod(block, EARLY_PER_PLANE)
            k, place = divmod(block - EARLY_BLOCKS, LATE_PER_PLANE)
            return k, EARLY_PER_PLANE + place

        load_x(0)

        nc.vector.memset(zeros[:].bitcast(I32), 0)
        warm = banks.tile([P, VOX], F32, name="acc")
        for i in range(WARM_PASSES):
            nc.tensor.matmul(out=warm[:], lhsT=zeros[:, 0:P], rhs=zeros[:], start=True, stop=True)

        nc.vector.memset(w_planes[:].bitcast(I32), 0)
        load_planes(0, EARLY_PER_PLANE, 0)
        load_w_columns(0, COUT // 2)
        load_w_columns(COUT // 2, COUT // 2)
        for d in (1, 2):
            load_w_direction(d)
        load_planes(EARLY_BLOCKS, LATE_PER_PLANE, EARLY_PER_PLANE)
        for d in (3, 4, 5, 6):
            load_w_direction(d)
        load_x(1)

        nc.vector.memset(centre_plane[:].bitcast(I32), 0)
        nc.vector.memset(centre_words[:, :, 0:SLAB], 0)
        nc.vector.memset(centre_words[:, :, SLAB + VOX :], 0)
        for shift in (-ROW, ROW):
            lo, hi = kept_range(shift, SLAB)
            slabs = moved_words[shift][:].rearrange("p b (t s) -> p (b t) s", s=SLAB)
            if lo > 0:
                nc.vector.memset(slabs[:, :, 0:lo], 0)
            else:
                nc.vector.memset(slabs[:, :, hi:SLAB], 0)
        for shift in (-1, 1):
            nc.vector.memset(moved_bf[shift][:].rearrange("p v j -> p (v j)").bitcast(I32), 0)

        def regroup_centre(copy, b, first, width):
            voxels = slice(first, first + width)
            copy(
                out=centre_bf[:, b, voxels, :].rearrange("p (g i) j -> p g j i", i=4),
                in_=raw[:, b, :, voxels].rearrange("p j (g i) -> p g j i", i=4),
            )

        def quantise_centre(b, first, width):
            voxels = slice(first, first + width)
            columns = slice(SLAB + first, SLAB + first + width)
            nc.vector.quantize_mx(
                out=centre_words[:, b, columns].bitcast(FP8X4),
                scales=centre_plane[:, b, columns],
                in_=centre_bf[:, b, voxels, :].rearrange("p v j -> p (v j)"),
            )

        def move_rows(b, shift):
            lo, hi = kept_range(shift, SLAB)
            source = centre_words[:, b, SLAB : SLAB + VOX].rearrange("p (t s) -> p t s", s=SLAB)
            target = moved_words[shift][:, b].rearrange("p (t s) -> p t s", s=SLAB)
            nc.vector.tensor_copy(out=target[:, :, lo:hi], in_=source[:, :, lo + shift : hi + shift])
            nc.vector.tensor_copy(
                out=moved_plane[shift][:, b].bitcast(I32),
                in_=centre_plane[:, b, SLAB + shift : SLAB + shift + VOX].bitcast(I32),
            )

        def move_columns(copy, b, shift):
            lo, hi = kept_range(shift, ROW)
            source = centre_bf[:, b].rearrange("p (s c) j -> p s (c j)", c=ROW)
            target = moved_bf[shift][:].rearrange("p (s c) j -> p s (c j)", c=ROW)
            copy(
                out=target[:, :, lo * PACK : hi * PACK],
                in_=source[:, :, (lo + shift) * PACK : (hi + shift) * PACK],
            )

        def quantise_moved(b, shift):
            nc.vector.quantize_mx(
                out=moved_words[shift][:, b].bitcast(FP8X4),
                scales=moved_plane[shift][:, b],
                in_=moved_bf[shift][:].rearrange("p v j -> p (v j)"),
            )

        def prepare(b, piece):
            for first in range(0, HALF, piece):
                regroup_centre(nc.vector.tensor_copy, b, first, piece)
            for first in range(HALF, VOX, piece):
                regroup_centre(nc.scalar.copy, b, first, piece)
            for first in range(0, VOX, piece):
                quantise_centre(b, first, piece)
            move_columns(nc.scalar.copy, b, -1)
            move_rows(b, -ROW)
            move_rows(b, ROW)
            move_columns(nc.vector.tensor_copy, b, 1)
            quantise_moved(b, -1)
            quantise_moved(b, 1)

        reads_from = (0, -SLAB, SLAB, -ROW, ROW, -1, 1)

        def mx_pass(acc_columns, b, m, d, first, width, start):
            shift = reads_from[d]
            if abs(shift) in (0, SLAB):
                window = slice(SLAB + shift + first, SLAB + shift + first + width)
                x_words, x_plane = centre_words[:, b, window], centre_plane[:, b, window]
            else:
                window = slice(first, first + width)
                x_words, x_plane = moved_words[shift][:, b, window], moved_plane[shift][:, b, window]
            block = d * M_TILES + m
            k, place = plane_of(block)
            nc.tensor.matmul_mx(
                out=acc_columns,
                lhsT=w_words[:, block * P : (block + 1) * P].bitcast(FP8X4),
                lhsT_scale=w_planes[4 * k : P, place * P : (place + 1) * P],
                rhs=x_words.bitcast(FP8X4),
                rhs_scale=x_plane,
                start=start,
                stop=(d == DIRECTIONS - 1),
            )

        def store(copy, acc, b, m, first, width):
            result = results.tile([P, width], F32, name="result", align_bytes=256)
            copy(out=result[:], in_=acc[:])
            out_rows = out[b, m * P : (m + 1) * P].rearrange("o t r c -> o (t r c)")
            nc.sync.dma_start(out=out_rows[:, first : first + width], in_=result[:])

        def first_direction(b, tiles, piece):
            for first in range(0, VOX, piece):
                for m in range(tiles):
                    mx_pass(accs[m][:, first : first + piece], b, m, 0, first, piece, first == 0)

        prepare(0, HALF // 2)
        accs = []
        for m in range(M_TILES):
            accs.append(banks.tile([P, VOX], F32, name="acc"))
        first_direction(0, M_TILES, HALF // 2)
        for d in range(1, DIRECTIONS - 2):
            for m in range(M_TILES):
                mx_pass(accs[m][:], 0, m, d, 0, VOX, False)
        prepare(1, HALF)
        for m in range(M_TILES):
            for d in range(DIRECTIONS - 2, DIRECTIONS):
                mx_pass(accs[m][:], 0, m, d, 0, VOX, False)
            store(nc.scalar.copy, accs[m], 0, m, 0, VOX)

        accs = []
        for m in range(M_TILES - 1):
            accs.append(banks.tile([P, VOX], F32, name="acc"))
        first_direction(1, M_TILES - 1, HALF)
        for d in range(1, DIRECTIONS - 2):
            for m in range(M_TILES - 1):
                mx_pass(accs[m][:], 1, m, d, 0, VOX, False)
        for m in range(M_TILES - 1):
            for d in range(DIRECTIONS - 2, DIRECTIONS):
                mx_pass(accs[m][:], 1, m, d, 0, VOX, False)
            store(nc.scalar.copy if m % 2 == 0 else nc.vector.tensor_copy, accs[m], 1, m, 0, VOX)
        for first, width in ((0, HALF), (HALF, HALF // 2), (HALF + HALF // 2, HALF // 2)):
            acc = banks.tile([P, width], F32, name="acc")
            for d in range(DIRECTIONS):
                mx_pass(acc[:], 1, M_TILES - 1, d, first, width, d == 0)
            last = first + width == VOX
            store(nc.vector.tensor_copy if last else nc.scalar.copy, acc, 1, M_TILES - 1, first, width)
